import numpy as np
import ml_dtypes


def mxq(x, axis, fmt="e4m3"):
    dtype, down = {"e4m3": (ml_dtypes.float8_e4m3fn, 7), "e5m2": (ml_dtypes.float8_e5m2, 14)}[fmt]
    v = np.moveaxis(np.asarray(x, np.float32).astype(ml_dtypes.bfloat16).astype(np.float64), axis, -1)
    blocks = v.reshape(v.shape[:-1] + (-1, 32))
    amax = np.abs(blocks).max(-1, keepdims=True)
    byte = np.maximum(np.where(amax > 0, np.frexp(amax)[1] - 1 + 127, 0) - down, 1)
    scale = np.exp2(byte - 127.0)
    codes = (blocks / scale).astype(np.float32).astype(dtype).astype(np.float64)
    return np.moveaxis((codes * scale).reshape(v.shape), -1, axis)


WIDE = False


def mx_kscale(k):
    if not WIDE:
        return np.ones(k)
    levels = np.array([10, -10, 5, -5, 0])
    if k % 512:
        return np.exp2(np.random.permutation(np.resize(levels, k // 32))).repeat(32)
    a = np.empty((k // 512, 16))
    for p in range(k // 512):
        a[p, :8] = np.random.permutation(np.resize(levels, 8))
        for g in range(8):
            far = levels[np.abs(levels - a[p, g]) >= 10]
            a[p, g + 8] = far[np.random.randint(len(far))]
    return np.exp2(a.ravel()).repeat(32)


BF16 = ml_dtypes.bfloat16


def bf(x):
    return np.asarray(x, np.float32).astype(BF16)


def f64(x):
    return np.asarray(x).astype(np.float64)


B, H, W, FI, FO = 4, 32, 32, 512, 1024

OFFSETS = [(-1, 0), (1, 0), (0, -1), (0, 1), (-1, -1), (-1, 1), (1, -1), (1, 1)]


def setup_inputs():
    s = mx_kscale(FI)
    return {"X": bf(np.random.standard_normal((B, H * W, FI)) * 0.5 * s),
            "Wm": bf(np.random.standard_normal((FI, FO)) / np.sqrt(FI) / s[:, None]),
            "b": bf(np.random.standard_normal(FO) * 0.2),
            "H": H, "W": W}


def reference(X, Wm, b, H, W):
    X = f64(X)
    Bn, N, F = X.shape
    Xg = X.reshape(Bn, H, W, F)
    P = np.pad(Xg, ((0, 0), (1, 1), (1, 1), (0, 0)))
    AX = P[:, 1 + OFFSETS[0][0]:1 + OFFSETS[0][0] + H,
           1 + OFFSETS[0][1]:1 + OFFSETS[0][1] + W, :]
    for dr, dc in OFFSETS[1:]:
        AX = AX + P[:, 1 + dr:1 + dr + H, 1 + dc:1 + dc + W, :]
    AX = AX.reshape(Bn, N, F)
    return (mxq(AX, 2, "e4m3") @ mxq(f64(Wm), 0, "e4m3")) + f64(b)

@@ -1,0 +1,303 @@
+from contextlib import ExitStack
+
+import concourse.mybir as mybir
+from concourse.masks import make_identity
+
+BF16 = mybir.dt.bfloat16
+F32 = mybir.dt.float32
+U32 = mybir.dt.uint32
+U8 = mybir.dt.uint8
+FP8X4 = mybir.dt.float8_e4m3fn_x4
+ADD = mybir.AluOpType.add
+
+P = 128
+FLOPS = 2 * 4096 * 512 * 1024
+
+PAIR_KINDS = "AAABABABABABABBB"
+G_HALVES = (0,)
+
+
+def tile_graphconvlayer_kernel(tc, X, Wm, b, H, W, out):
+    nc = tc.nc
+    n_feat = X.shape[2]
+    n_out = Wm.shape[1]
+    n_t = n_feat // P
+    w_view = Wm.rearrange("(p t) n -> p t n", t=n_t)
+    z_img = 3
+    xz_view = X[z_img].rearrange("(p i) f -> p i f", i=8)
+    xz_rows = X[z_img].rearrange("(r k) f -> r k f", k=32)
+    oz_view = out[z_img].rearrange("(p i) n -> p i n", i=8)
+
+    with ExitStack() as ctx:
+        const = ctx.enter_context(tc.tile_pool(name="const", bufs=1))
+        ts_pool = ctx.enter_context(tc.tile_pool(name="ts", bufs=4))
+        work = ctx.enter_context(tc.tile_pool(name="work", bufs=2))
+        stage = ctx.enter_context(tc.tile_pool(name="stage", bufs=8))
+        ps_a = ctx.enter_context(tc.psum_pool(name="ps_a", bufs=2))
+        ps_o = ctx.enter_context(tc.psum_pool(name="ps_o", bufs=4))
+        ctx.enter_context(tc.manual_schedule())
+
+        x0 = const.tile([P, 24, n_feat], BF16)
+        x2 = const.tile([P, 21, n_feat], BF16)
+        xz = const.tile([P, 10, n_feat], BF16)
+        xf = const.tile([P, 2, n_feat], BF16)
+        w_raw = const.tile([P, n_t, n_out], BF16)
+        b_bc = const.tile([P, n_out], BF16)
+        id32 = const.tile([P, P], F32)
+        idx = const.tile([P, 32], F32, align_bytes=64)
+        low = const.tile([P, 32], F32, align_bytes=64)
+        dif = const.tile([P, 32], F32)
+        sq = const.tile([P, 32], F32)
+        pat = const.tile([P, 96], BF16)
+        blk = const.tile([P, 32], F32)
+        adj = const.tile([P, 192], BF16)
+        cyc_up = const.tile([P, P], F32)
+        cyc_dn = const.tile([P, P], F32)
+        w_grp = const.tile([P, n_out, n_t], BF16, align_bytes=64)
+        w_q = const.tile([P, n_out], U32, align_bytes=64)
+        w_s = const.tile([P, n_out], U8, align_bytes=64)
+        bias = const.tile([P, n_out], F32)
+        fix = const.tile([P, 8, 2, 4, n_t], BF16)
+
+        def load_x0(img, lo, hi):
+            nc.sync.dma_start(out=x0[:, 8 * img + lo:8 * img + hi, :],
+                              in_=X[img, P * lo:P * hi, :].rearrange("(j p) f -> p j f", p=P))
+
+        def load_x2(img, lo, hi):
+            nc.sync.dma_start(out=x2[:, 7 * img + lo:7 * img + hi, :],
+                              in_=X[img, 64 + P * lo:64 + P * hi, :].rearrange("(j p) f -> p j f", p=P))
+
+        nc.vector.memset(xz[:, 0, :], 0.0)
+        nc.vector.memset(xz[:, 9, :], 0.0)
+        load_x0(0, 0, 2)
+        load_x2(0, 0, 2)
+        nc.sync.dma_start(out=w_raw[:, :, 0:512], in_=w_view[:, :, 0:512])
+        nc.sync.dma_start(out=w_raw[:, :, 512:1024], in_=w_view[:, :, 512:1024])
+        nc.scalar.dma_start(out=b_bc[:], in_=b.partition_broadcast(P))
+        load_x0(0, 2, 4)
+        load_x2(0, 2, 4)
+        load_x0(0, 4, 8)
+        load_x2(0, 4, 7)
+        nc.sync.dma_start(out=xz[:, 1:5, :], in_=xz_view[:, 0:4, :])
+        for cq in range(1, 4):
+            nc.sync.dma_start(out=xz[cq:128:4, 0, :], in_=xz_rows[:, 8 * cq - 1, :])
+        nc.sync.dma_start(out=xf[:, 0, :], in_=X[z_img, 0:128, :])
+        nc.sync.dma_start(out=xf[:, 1, :], in_=X[z_img, 896:1024, :])
+        load_x0(1, 0, 4)
+        load_x2(1, 0, 4)
+        nc.sync.dma_start(out=xz[:, 5:9, :], in_=xz_view[:, 4:8, :])
+        for cq in range(0, 3):
+            nc.sync.dma_start(out=xz[cq:128:4, 9, :], in_=xz_rows[:, 8 * cq + 8, :])
+
+        later_loads = {0: (1, 1), 2: (2, 0), 5: (2, 1)}
+
+        def load_half_image(img, half):
+            load_x0(img, 4 * half, 4 * half + 4)
+            load_x2(img, 4 * half, min(4 * half + 4, 7))
+
+        nc.vector.memset(adj[:], 0.0)
+        nc.vector.memset(id32[:], 0.0)
+        nc.vector.memset(idx[:, 0:1], 0.0)
+        for w in (1, 2, 4, 8, 16):
+            nc.vector.tensor_scalar_add(out=idx[:, w:2 * w], in0=idx[:, 0:w], scalar1=float(w))
+        nc.vector.transpose(out=low[:], in_=idx[:])
+        nc.vector.tensor_scalar(out=dif[:], in0=idx[:], scalar1=low[:, 0:1], scalar2=None,
+                                op0=mybir.AluOpType.subtract)
+        nc.vector.tensor_tensor(out=sq[:], in0=dif[:], in1=dif[:], op=mybir.AluOpType.mult)
+        nc.vector.tensor_scalar(out=pat[:, 0:32], in0=sq[:], scalar1=1.0, scalar2=None, op0=mybir.AluOpType.is_le)
+        nc.vector.tensor_scalar(out=pat[:, 32:64], in0=sq[:], scalar1=1.0, scalar2=None, op0=mybir.AluOpType.is_equal)
+        nc.vector.tensor_scalar(out=pat[:, 64:96], in0=sq[:], scalar1=1.0, scalar2=None, op0=mybir.AluOpType.is_le)
+        for rl in range(4):
+            rows = slice(32 * rl, 32 * rl + 32)
+            nc.vector.tensor_copy(out=adj[rows, 32 * rl:32 * rl + 96], in_=pat[rows, :])
+
+        def regroup(copy, lo, hi):
+            copy(out=w_grp[:, lo:hi, :], in_=w_raw[:, :, lo:hi].rearrange("p t n -> p n t"))
+
+        def weights_q(h):
+            cols = slice(512 * h, 512 * h + 512)
+            nc.vector.quantize_mx(out=w_q[:, cols].bitcast(FP8X4), scales=w_s[:, cols],
+                                  in_=w_grp[:, cols, :].rearrange("p n t -> p (n t)"))
+
+        def shifts():
+            nc.vector.tensor_scalar(out=blk[:], in0=sq[:], scalar1=0.0, scalar2=None, op0=mybir.AluOpType.is_equal)
+            for q in range(4):
+                rows = slice(32 * q, 32 * q + 32)
+                nc.vector.tensor_copy(out=id32[rows, 32 * q:32 * q + 32], in_=blk[rows, :])
+            nc.vector.tensor_copy(out=cyc_up[:, 4:128], in_=id32[:, 0:124])
+            nc.vector.tensor_copy(out=cyc_up[:, 0:4], in_=id32[:, 124:128])
+            nc.vector.tensor_copy(out=cyc_dn[:, 0:124], in_=id32[:, 4:128])
+            nc.vector.tensor_copy(out=cyc_dn[:, 124:128], in_=id32[:, 0:4])
+
+        def border_rows_sum():
+            acc_f = ps_a.tile([P, n_t, P], F32, tag="acc1")
+            for t in range(n_t):
+                f = slice(t, n_feat, n_t)
+                nc.tensor.matmul(acc_f[:, t, 0:32], lhsT=xf[:, 0, f], rhs=adj[:, 32:64], start=True, stop=True)
+                nc.tensor.matmul(acc_f[:, t, 32:64], lhsT=xf[:, 1, f], rhs=adj[:, 128:160], start=True, stop=True)
+            return acc_f
+
+        def border_rows_round(acc_f):
+            for rr in range(2):
+                nc.scalar.copy(out=fix[:, :, rr, :, :],
+                               in_=acc_f[:, :, 32 * rr:32 * rr + 32].rearrange("p t (q i) -> p i q t", q=4))
+
+        def row_sums(ci):
+            t32 = ts_pool.tile([P, n_feat], F32, tag="t32")
+            s32 = ts_pool.tile([P, n_feat], F32, tag="s32")
+            by_t = lambda row: row.rearrange("p (m t) -> p t m", t=n_t)
+            t_out = t32[:].rearrange("p (t m) -> p t m", t=n_t)
+            s_out = s32[:].rearrange("p (t m) -> p t m", t=n_t)
+            nc.vector.tensor_tensor(out=t_out, in0=by_t(xz[:, ci, :]), in1=by_t(xz[:, ci + 2, :]), op=ADD)
+            nc.vector.tensor_tensor(out=s_out, in0=t_out, in1=by_t(xz[:, ci + 1, :]), op=ADD)
+            return t32, s32
+
+        def z_sum(acc, t32, s32):
+            for t in range(n_t):
+                f = slice(P * t, P * t + P)
+                nc.tensor.matmul(acc[:, t, :], lhsT=t32[:, f], rhs=id32[:], is_transpose=True, start=True, stop=False)
+                nc.tensor.matmul(acc[:, t, :], lhsT=s32[:, f], rhs=cyc_up[:], is_transpose=True, start=False, stop=False)
+                nc.tensor.matmul(acc[:, t, :], lhsT=s32[:, f], rhs=cyc_dn[:], is_transpose=True, start=False, stop=True)
+
+        def p_parts(n):
+            img = n // 8
+            u = n % 8
+            if u < 7:
+                return [(x0, 8 * img + u, 64, 0, 64), (x2, 7 * img + u, 64, 64, 64)]
+            return [(x0, 8 * img, 32, 0, 32), (x0, 8 * img + 7, 64, 32, 64), (x0, 8 * img + 7, 128, 96, 32)]
+
+        def p_sum(acc, n):
+            for t in range(n_t):
+                f = slice(t, n_feat, n_t)
+                for (src, blk, a_lo, o_lo, width) in p_parts(n):
+                    nc.tensor.matmul(acc[:, t, o_lo:o_lo + width], lhsT=src[:, blk, f], rhs=adj[:, a_lo:a_lo + width],
+                                     start=True, stop=True)
+
+        def p_stores(n):
+            img = n // 8
+            u = n % 8
+            if u < 7:
+                return [(0, P, out[img, P * u + 32:P * u + 160, :])]
+            return [(0, 32, out[img, 0:32, :]), (32, 96, out[img, 928:992, :]), (96, P, out[img, 992:1024, :])]
+
+        pairs = []
+        first_use = {}
+        n_p = 0
+        n_z = 0
+        for s, kind in enumerate(PAIR_KINDS):
+            if kind == "A":
+                pairs.append([("p", n_p), ("p", n_p + 1)])
+                n_p += 2
+            else:
+                pairs.append([("p", n_p), ("z", n_z)])
+                first_use[s] = n_z
+                n_p += 1
+                n_z += 1
+
+        def pair_tiles(s):
+            return pairs[s]
+
+        def neighbour_sums(s, sums):
+            accs = []
+            for a, (kind, n) in enumerate(pair_tiles(s)):
+                acc = ps_a.tile([P, n_t, P], F32, tag="acc%d" % a, name="acc%d" % a)
+                if kind == "p":
+                    p_sum(acc, n)
+                else:
+                    z_sum(acc, sums[n][0], sums[n][1])
+                accs.append(acc)
+            return accs
+
+        def round_out(s, a, accs, grp):
+            kind, n = pair_tiles(s)[a]
+            nc.scalar.copy(out=grp[:, a, :, :], in_=accs[a][:].rearrange("p t n -> p n t"))
+            if kind == "z":
+                nc.scalar.copy(out=grp[:, a, 0:4, :], in_=fix[:, n, 0, :, :])
+                nc.scalar.copy(out=grp[:, a, 124:128, :], in_=fix[:, n, 1, :, :])
+
+        def quantise(grp):
+            a_q = work.tile([P, 2 * P], U32, align_bytes=64, tag="a_q")
+            a_s = work.tile([P, 2 * P], U8, align_bytes=64, tag="a_s")
+            nc.vector.quantize_mx(out=a_q[:].bitcast(FP8X4), scales=a_s[:],
+                                  in_=grp[:].rearrange("p a n t -> p (a n t)"))
+            return a_q, a_s
+
+        def multiply(a_q, a_s):
+            banks = []
+            for h in range(2):
+                cols = slice(512 * h, 512 * h + 512)
+                for a in range(2):
+                    nodes = slice(P * a, P * a + P)
+                    po = ps_o.tile([P, 512], F32, tag="po", name="po%d%d" % (h, a))
+                    nc.tensor.matmul_mx(out=po[:], lhsT=a_q[:, nodes].bitcast(FP8X4), lhsT_scale=a_s[:, nodes],
+                                        rhs=w_q[:, cols].bitcast(FP8X4), rhs_scale=w_s[:, cols],
+                                        start=True, stop=True)
+                    banks.append(po)
+            return banks
+
+        def out_tiles():
+            o_tiles = []
+            for a in range(2):
+                o_new = stage.tile([P, n_out], F32, tag="o_sb", name="o_sb%d" % a)
+                o_tiles.append(o_new)
+            return o_tiles
+
+        def add_bias(k, banks, o_tiles):
+            cols = slice(512 * (k // 2), 512 * (k // 2) + 512)
+            o_sb = o_tiles[k % 2]
+            if k in G_HALVES:
+                nc.scalar.copy(out=o_sb[:, cols], in_=banks[k][:])
+                nc.gpsimd.tensor_tensor(out=o_sb[:, cols], in0=o_sb[:, cols], in1=bias[:, cols], op=ADD)
+            else:
+                nc.vector.tensor_tensor(out=o_sb[:, cols], in0=banks[k][:], in1=bias[:, cols], op=ADD)
+
+        def store(s, a, o_tiles):
+            kind, n = pair_tiles(s)[a]
+            if kind == "z":
+                nc.sync.dma_start(out=oz_view[:, n, :], in_=o_tiles[a][:])
+            else:
+                for (lo, hi, dest) in p_stores(n):
+                    nc.sync.dma_start(out=dest, in_=o_tiles[a][lo:hi, :])
+
+        n_pairs = len(PAIR_KINDS)
+        sums = {}
+        shifts()
+        regroup(nc.vector.tensor_copy, 0, 512)
+        weights_q(0)
+        accs = neighbour_sums(0, sums)
+        grp_next = work.tile([P, 2, P, n_t], BF16, align_bytes=64, tag="grp")
+        round_out(0, 0, accs, grp_next)
+        round_out(0, 1, accs, grp_next)
+        regroup(nc.scalar.copy, 768, 1024)
+        nc.scalar.copy(out=bias[:], in_=b_bc[:])
+        regroup(nc.vector.tensor_copy, 512, 768)
+        ready = quantise(grp_next)
+        weights_q(1)
+        sums_after = {}
+        for s in sorted(first_use):
+            sums_after[max(s - 4, 0)] = first_use[s]
+        for s in range(n_pairs):
+            more = s + 1 < n_pairs
+            if more:
+                accs = neighbour_sums(s + 1, sums)
+            banks = multiply(ready[0], ready[1])
+            if s == 1:
+                acc_f = border_rows_sum()
+            o_tiles = out_tiles()
+            if more:
+                grp_next = work.tile([P, 2, P, n_t], BF16, align_bytes=64, tag="grp")
+                round_out(s + 1, 0, accs, grp_next)
+                round_out(s + 1, 1, accs, grp_next)
+                ready = quantise(grp_next)
+            add_bias(0, banks, o_tiles)
+            if s == 1:
+                border_rows_round(acc_f)
+            add_bias(1, banks, o_tiles)
+            add_bias(2, banks, o_tiles)
+            store(s, 0, o_tiles)
+            add_bias(3, banks, o_tiles)
+            store(s, 1, o_tiles)
+            if s in later_loads:
+                load_half_image(later_loads[s][0], later_loads[s][1])
+            if s in sums_after:
+                sums[sums_after[s]] = row_sums(sums_after[s])

@@ -40,7 +40,7 @@ def tile_graphconvlayer_kernel(tc, X, Wm, b, H, W, out):
         x0 = const.tile([P, 24, n_feat], BF16)
         x2 = const.tile([P, 21, n_feat], BF16)
         xz = const.tile([P, 10, n_feat], BF16)
-        xf = const.tile([P, 2, n_feat], BF16)
+        xf = const.tile([P, n_feat], BF16)
         w_raw = const.tile([P, n_t, n_out], BF16)
         b_bc = const.tile([P, n_out], BF16)
         id32 = const.tile([P, P], F32)
@@ -50,41 +50,38 @@ def tile_graphconvlayer_kernel(tc, X, Wm, b, H, W, out):
         sq = const.tile([P, 32], F32)
         pat = const.tile([P, 96], BF16)
         blk = const.tile([P, 32], F32)
-        adj = const.tile([P, 192], BF16)
+        adj = const.tile([P, 256], BF16)
         cyc_up = const.tile([P, P], F32)
         cyc_dn = const.tile([P, P], F32)
         w_grp = const.tile([P, n_out, n_t], BF16, align_bytes=64)
         w_q = const.tile([P, n_out], U32, align_bytes=64)
         w_s = const.tile([P, n_out], U8, align_bytes=64)
-        bias = const.tile([P, n_out], F32)
         fix = const.tile([P, 8, 2, 4, n_t], BF16)
 
         def load_x0(img, lo, hi):
             nc.sync.dma_start(out=x0[:, 8 * img + lo:8 * img + hi, :],
                               in_=X[img, P * lo:P * hi, :].rearrange("(j p) f -> p j f", p=P))
 
-        def load_x2(img, lo, hi):
-            nc.sync.dma_start(out=x2[:, 7 * img + lo:7 * img + hi, :],
-                              in_=X[img, 64 + P * lo:64 + P * hi, :].rearrange("(j p) f -> p j f", p=P))
+        def fill_x2(copy, img, lo, hi):
+            to = slice(7 * img + lo, 7 * img + hi)
+            copy(out=x2[0:64, to, :], in_=x0[0:64, 8 * img + lo + 1:8 * img + hi + 1, :])
+            copy(out=x2[64:128, to, :], in_=x0[64:128, 8 * img + lo:8 * img + hi, :])
 
-        nc.vector.memset(xz[:, 0, :], 0.0)
-        nc.vector.memset(xz[:, 9, :], 0.0)
-        load_x0(0, 0, 2)
-        load_x2(0, 0, 2)
+        nc.gpsimd.memset(adj[:], 0.0)
+        nc.gpsimd.memset(id32[:], 0.0)
+        nc.gpsimd.memset(xz[:, 0, :], 0.0)
+        nc.gpsimd.memset(xz[:, 9, :], 0.0)
+        load_x0(0, 0, 3)
         nc.sync.dma_start(out=w_raw[:, :, 0:512], in_=w_view[:, :, 0:512])
         nc.sync.dma_start(out=w_raw[:, :, 512:1024], in_=w_view[:, :, 512:1024])
         nc.scalar.dma_start(out=b_bc[:], in_=b.partition_broadcast(P))
-        load_x0(0, 2, 4)
-        load_x2(0, 2, 4)
-        load_x0(0, 4, 8)
-        load_x2(0, 4, 7)
+        load_x0(0, 3, 8)
         nc.sync.dma_start(out=xz[:, 1:5, :], in_=xz_view[:, 0:4, :])
         for cq in range(1, 4):
             nc.sync.dma_start(out=xz[cq:128:4, 0, :], in_=xz_rows[:, 8 * cq - 1, :])
-        nc.sync.dma_start(out=xf[:, 0, :], in_=X[z_img, 0:128, :])
-        nc.sync.dma_start(out=xf[:, 1, :], in_=X[z_img, 896:1024, :])
+        nc.sync.dma_start(out=xf[0:64, :], in_=X[z_img, 0:64, :])
+        nc.sync.dma_start(out=xf[64:128, :], in_=X[z_img, 960:1024, :])
         load_x0(1, 0, 4)
-        load_x2(1, 0, 4)
         nc.sync.dma_start(out=xz[:, 5:9, :], in_=xz_view[:, 4:8, :])
         for cq in range(0, 3):
             nc.sync.dma_start(out=xz[cq:128:4, 9, :], in_=xz_rows[:, 8 * cq + 8, :])
@@ -93,10 +90,7 @@ def tile_graphconvlayer_kernel(tc, X, Wm, b, H, W, out):
 
         def load_half_image(img, half):
             load_x0(img, 4 * half, 4 * half + 4)
-            load_x2(img, 4 * half, min(4 * half + 4, 7))
 
-        nc.vector.memset(adj[:], 0.0)
-        nc.vector.memset(id32[:], 0.0)
         nc.vector.memset(idx[:, 0:1], 0.0)
         for w in (1, 2, 4, 8, 16):
             nc.vector.tensor_scalar_add(out=idx[:, w:2 * w], in0=idx[:, 0:w], scalar1=float(w))
@@ -110,6 +104,11 @@ def tile_graphconvlayer_kernel(tc, X, Wm, b, H, W, out):
         for rl in range(4):
             rows = slice(32 * rl, 32 * rl + 32)
             nc.vector.tensor_copy(out=adj[rows, 32 * rl:32 * rl + 96], in_=pat[rows, :])
+        nc.vector.tensor_copy(out=adj[0:32, 192:256], in_=pat[0:32, 0:64])
+        nc.vector.tensor_copy(out=adj[32:64, 224:256], in_=pat[32:64, 0:32])
+        nc.vector.tensor_copy(out=adj[64:96, 192:224], in_=pat[64:96, 64:96])
+        nc.vector.tensor_copy(out=adj[96:128, 192:256], in_=pat[96:128, 32:96])
+        fill_x2(nc.vector.tensor_copy, 0, 0, 2)
 
         def regroup(copy, lo, hi):
             copy(out=w_grp[:, lo:hi, :], in_=w_raw[:, :, lo:hi].rearrange("p t n -> p n t"))
@@ -130,11 +129,11 @@ def tile_graphconvlayer_kernel(tc, X, Wm, b, H, W, out):
             nc.vector.tensor_copy(out=cyc_dn[:, 124:128], in_=id32[:, 0:4])
 
         def border_rows_sum():
-            acc_f = ps_a.tile([P, n_t, P], F32, tag="acc1")
+            acc_f = ps_a.tile([P, n_t, P], F32, tag="accz")
             for t in range(n_t):
                 f = slice(t, n_feat, n_t)
-                nc.tensor.matmul(acc_f[:, t, 0:32], lhsT=xf[:, 0, f], rhs=adj[:, 32:64], start=True, stop=True)
-                nc.tensor.matmul(acc_f[:, t, 32:64], lhsT=xf[:, 1, f], rhs=adj[:, 128:160], start=True, stop=True)
+                nc.tensor.matmul(acc_f[:, t, 0:64], lhsT=xf[:, f],
+                                 rhs=adj[:, 0:192].rearrange("p (b j) -> p b j", b=6)[:, 1:5:3, :], start=True, stop=True)
             return acc_f
 
         def border_rows_round(acc_f):
@@ -163,14 +162,14 @@ def tile_graphconvlayer_kernel(tc, X, Wm, b, H, W, out):
             img = n // 8
             u = n % 8
             if u < 7:
-                return [(x0, 8 * img + u, 64, 0, 64), (x2, 7 * img + u, 64, 64, 64)]
-            return [(x0, 8 * img, 32, 0, 32), (x0, 8 * img + 7, 64, 32, 64), (x0, 8 * img + 7, 128, 96, 32)]
+                return [(x0, 8 * img + u, 64, 0, 64), (x2, 7 * img + u, 192, 64, 64)]
+            return [(x0, 8 * img, 32, 0, 32), (x0, 8 * img + 7, 64, 32, 96)]
 
-        def p_sum(acc, n):
+        def p_sum(acc, a, n):
             for t in range(n_t):
                 f = slice(t, n_feat, n_t)
                 for (src, blk, a_lo, o_lo, width) in p_parts(n):
-                    nc.tensor.matmul(acc[:, t, o_lo:o_lo + width], lhsT=src[:, blk, f], rhs=adj[:, a_lo:a_lo + width],
+                    nc.tensor.matmul(acc[:, a, t, o_lo:o_lo + width], lhsT=src[:, blk, f], rhs=adj[:, a_lo:a_lo + width],
                                      start=True, stop=True)
 
         def p_stores(n):
@@ -197,23 +196,33 @@ def tile_graphconvlayer_kernel(tc, X, Wm, b, H, W, out):
         def pair_tiles(s):
             return pairs[s]
 
-        def neighbour_sums(s, sums):
-            accs = []
-            for a, (kind, n) in enumerate(pair_tiles(s)):
-                acc = ps_a.tile([P, n_t, P], F32, tag="acc%d" % a, name="acc%d" % a)
-                if kind == "p":
-                    p_sum(acc, n)
-                else:
-                    z_sum(acc, sums[n][0], sums[n][1])
-                accs.append(acc)
-            return accs
+        def strips_of(s):
+            tiles = [(n // 8, n % 8) for kind, n in pair_tiles(s) if kind == "p" and n % 8 < 7]
+            if len(tiles) == 2 and tiles[0][0] == tiles[1][0]:
+                return [(tiles[0][0], tiles[0][1], tiles[1][1] + 1)]
+            return [(img, u, u + 1) for img, u in tiles]
 
-        def round_out(s, a, accs, grp):
-            kind, n = pair_tiles(s)[a]
-            nc.scalar.copy(out=grp[:, a, :, :], in_=accs[a][:].rearrange("p t n -> p n t"))
-            if kind == "z":
-                nc.scalar.copy(out=grp[:, a, 0:4, :], in_=fix[:, n, 0, :, :])
-                nc.scalar.copy(out=grp[:, a, 124:128, :], in_=fix[:, n, 1, :, :])
+        def neighbour_sums(s, sums):
+            acc_p = ps_a.tile([P, 2, n_t, P], BF16, tag="accp")
+            acc_z = None
+            for a, (kind, n) in enumerate(pair_tiles(s)):
+                if kind == "p":
+                    p_sum(acc_p, a, n)
+                else:
+                    acc_z = ps_a.tile([P, n_t, P], F32, tag="accz")
+                    z_sum(acc_z, sums[n][0], sums[n][1])
+            return acc_p, acc_z
+
+        def round_out(s, accs, grp):
+            acc_p, acc_z = accs
+            if acc_z is None:
+                nc.scalar.copy(out=grp[:], in_=acc_p[:].rearrange("p a t n -> p a n t"))
+            else:
+                n = pair_tiles(s)[1][1]
+                nc.scalar.copy(out=grp[:, 0, :, :], in_=acc_p[:, 0, :, :].rearrange("p t n -> p n t"))
+                nc.scalar.copy(out=grp[:, 1, :, :], in_=acc_z[:].rearrange("p t n -> p n t"))
+                nc.scalar.copy(out=grp[:, 1, 0:4, :], in_=fix[:, n, 0, :, :])
+                nc.scalar.copy(out=grp[:, 1, 124:128, :], in_=fix[:, n, 1, :, :])
 
         def quantise(grp):
             a_q = work.tile([P, 2 * P], U32, align_bytes=64, tag="a_q")
@@ -247,9 +256,9 @@ def tile_graphconvlayer_kernel(tc, X, Wm, b, H, W, out):
             o_sb = o_tiles[k % 2]
             if k in G_HALVES:
                 nc.scalar.copy(out=o_sb[:, cols], in_=banks[k][:])
-                nc.gpsimd.tensor_tensor(out=o_sb[:, cols], in0=o_sb[:, cols], in1=bias[:, cols], op=ADD)
+                nc.gpsimd.tensor_tensor(out=o_sb[:, cols], in0=o_sb[:, cols], in1=b_bc[:, cols], op=ADD)
             else:
-                nc.vector.tensor_tensor(out=o_sb[:, cols], in0=banks[k][:], in1=bias[:, cols], op=ADD)
+                nc.vector.tensor_tensor(out=o_sb[:, cols], in0=banks[k][:], in1=b_bc[:, cols], op=ADD)
 
         def store(s, a, o_tiles):
             kind, n = pair_tiles(s)[a]
@@ -266,10 +275,10 @@ def tile_graphconvlayer_kernel(tc, X, Wm, b, H, W, out):
         weights_q(0)
         accs = neighbour_sums(0, sums)
         grp_next = work.tile([P, 2, P, n_t], BF16, align_bytes=64, tag="grp")
-        round_out(0, 0, accs, grp_next)
-        round_out(0, 1, accs, grp_next)
+        round_out(0, accs, grp_next)
+        fill_x2(nc.scalar.copy, 0, 2, 4)
         regroup(nc.scalar.copy, 768, 1024)
-        nc.scalar.copy(out=bias[:], in_=b_bc[:])
+        fill_x2(nc.scalar.copy, 0, 4, 6)
         regroup(nc.vector.tensor_copy, 512, 768)
         ready = quantise(grp_next)
         weights_q(1)
@@ -286,10 +295,12 @@ def tile_graphconvlayer_kernel(tc, X, Wm, b, H, W, out):
             o_tiles = out_tiles()
             if more:
                 grp_next = work.tile([P, 2, P, n_t], BF16, align_bytes=64, tag="grp")
-                round_out(s + 1, 0, accs, grp_next)
-                round_out(s + 1, 1, accs, grp_next)
+                round_out(s + 1, accs, grp_next)
                 ready = quantise(grp_next)
             add_bias(0, banks, o_tiles)
+            if s + 3 < n_pairs:
+                for (img, lo, hi) in strips_of(s + 3):
+                    fill_x2(nc.scalar.copy, img, lo, hi)
             if s == 1:
                 border_rows_round(acc_f)
             add_bias(1, banks, o_tiles)

from contextlib import ExitStack

import concourse.mybir as mybir
from concourse.masks import make_identity

BF16 = mybir.dt.bfloat16
F32 = mybir.dt.float32
U32 = mybir.dt.uint32
U8 = mybir.dt.uint8
FP8X4 = mybir.dt.float8_e4m3fn_x4
ADD = mybir.AluOpType.add

P = 128
FLOPS = 2 * 4096 * 512 * 1024

PAIR_KINDS = "AAABABABABABABBB"
G_HALVES = (0,)


def tile_graphconvlayer_kernel(tc, X, Wm, b, H, W, out):
    nc = tc.nc
    n_feat = X.shape[2]
    n_out = Wm.shape[1]
    n_t = n_feat // P
    w_view = Wm.rearrange("(p t) n -> p t n", t=n_t)
    z_img = 3
    xz_view = X[z_img].rearrange("(p i) f -> p i f", i=8)
    xz_rows = X[z_img].rearrange("(r k) f -> r k f", k=32)
    oz_view = out[z_img].rearrange("(p i) n -> p i n", i=8)

    with ExitStack() as ctx:
        const = ctx.enter_context(tc.tile_pool(name="const", bufs=1))
        ts_pool = ctx.enter_context(tc.tile_pool(name="ts", bufs=4))
        work = ctx.enter_context(tc.tile_pool(name="work", bufs=2))
        stage = ctx.enter_context(tc.tile_pool(name="stage", bufs=8))
        ps_a = ctx.enter_context(tc.psum_pool(name="ps_a", bufs=2))
        ps_o = ctx.enter_context(tc.psum_pool(name="ps_o", bufs=4))
        ctx.enter_context(tc.manual_schedule())

        x0 = const.tile([P, 24, n_feat], BF16)
        x2 = const.tile([P, 21, n_feat], BF16)
        xz = const.tile([P, 10, n_feat], BF16)
        xf = const.tile([P, n_feat], BF16)
        w_raw = const.tile([P, n_t, n_out], BF16)
        b_bc = const.tile([P, n_out], BF16)
        id32 = const.tile([P, P], F32)
        idx = const.tile([P, 32], F32, align_bytes=64)
        low = const.tile([P, 32], F32, align_bytes=64)
        dif = const.tile([P, 32], F32)
        sq = const.tile([P, 32], F32)
        pat = const.tile([P, 96], BF16)
        blk = const.tile([P, 32], F32)
        adj = const.tile([P, 256], BF16)
        cyc_up = const.tile([P, P], F32)
        cyc_dn = const.tile([P, P], F32)
        w_grp = const.tile([P, n_out, n_t], BF16, align_bytes=64)
        w_q = const.tile([P, n_out], U32, align_bytes=64)
        w_s = const.tile([P, n_out], U8, align_bytes=64)
        fix = const.tile([P, 8, 2, 4, n_t], BF16)

        def load_x0(img, lo, hi):
            nc.sync.dma_start(out=x0[:, 8 * img + lo:8 * img + hi, :],
                              in_=X[img, P * lo:P * hi, :].rearrange("(j p) f -> p j f", p=P))

        def fill_x2(copy, img, lo, hi):
            to = slice(7 * img + lo, 7 * img + hi)
            copy(out=x2[0:64, to, :], in_=x0[0:64, 8 * img + lo + 1:8 * img + hi + 1, :])
            copy(out=x2[64:128, to, :], in_=x0[64:128, 8 * img + lo:8 * img + hi, :])

        nc.gpsimd.memset(adj[:], 0.0)
        nc.gpsimd.memset(id32[:], 0.0)
        nc.gpsimd.memset(xz[:, 0, :], 0.0)
        nc.gpsimd.memset(xz[:, 9, :], 0.0)
        load_x0(0, 0, 3)
        nc.sync.dma_start(out=w_raw[:, :, 0:512], in_=w_view[:, :, 0:512])
        nc.sync.dma_start(out=w_raw[:, :, 512:1024], in_=w_view[:, :, 512:1024])
        nc.scalar.dma_start(out=b_bc[:], in_=b.partition_broadcast(P))
        load_x0(0, 3, 8)
        nc.sync.dma_start(out=xz[:, 1:5, :], in_=xz_view[:, 0:4, :])
        for cq in range(1, 4):
            nc.sync.dma_start(out=xz[cq:128:4, 0, :], in_=xz_rows[:, 8 * cq - 1, :])
        nc.sync.dma_start(out=xf[0:64, :], in_=X[z_img, 0:64, :])
        nc.sync.dma_start(out=xf[64:128, :], in_=X[z_img, 960:1024, :])
        load_x0(1, 0, 4)
        nc.sync.dma_start(out=xz[:, 5:9, :], in_=xz_view[:, 4:8, :])
        for cq in range(0, 3):
            nc.sync.dma_start(out=xz[cq:128:4, 9, :], in_=xz_rows[:, 8 * cq + 8, :])

        later_loads = {0: (1, 1), 2: (2, 0), 5: (2, 1)}

        def load_half_image(img, half):
            load_x0(img, 4 * half, 4 * half + 4)

        nc.vector.memset(idx[:, 0:1], 0.0)
        for w in (1, 2, 4, 8, 16):
            nc.vector.tensor_scalar_add(out=idx[:, w:2 * w], in0=idx[:, 0:w], scalar1=float(w))
        nc.vector.transpose(out=low[:], in_=idx[:])
        nc.vector.tensor_scalar(out=dif[:], in0=idx[:], scalar1=low[:, 0:1], scalar2=None,
                                op0=mybir.AluOpType.subtract)
        nc.vector.tensor_tensor(out=sq[:], in0=dif[:], in1=dif[:], op=mybir.AluOpType.mult)
        nc.vector.tensor_scalar(out=pat[:, 0:32], in0=sq[:], scalar1=1.0, scalar2=None, op0=mybir.AluOpType.is_le)
        nc.vector.tensor_scalar(out=pat[:, 32:64], in0=sq[:], scalar1=1.0, scalar2=None, op0=mybir.AluOpType.is_equal)
        nc.vector.tensor_scalar(out=pat[:, 64:96], in0=sq[:], scalar1=1.0, scalar2=None, op0=mybir.AluOpType.is_le)
        for rl in range(4):
            rows = slice(32 * rl, 32 * rl + 32)
            nc.vector.tensor_copy(out=adj[rows, 32 * rl:32 * rl + 96], in_=pat[rows, :])
        nc.vector.tensor_copy(out=adj[0:32, 192:256], in_=pat[0:32, 0:64])
        nc.vector.tensor_copy(out=adj[32:64, 224:256], in_=pat[32:64, 0:32])
        nc.vector.tensor_copy(out=adj[64:96, 192:224], in_=pat[64:96, 64:96])
        nc.vector.tensor_copy(out=adj[96:128, 192:256], in_=pat[96:128, 32:96])
        fill_x2(nc.vector.tensor_copy, 0, 0, 2)

        def regroup(copy, lo, hi):
            copy(out=w_grp[:, lo:hi, :], in_=w_raw[:, :, lo:hi].rearrange("p t n -> p n t"))

        def weights_q(h):
            cols = slice(512 * h, 512 * h + 512)
            nc.vector.quantize_mx(out=w_q[:, cols].bitcast(FP8X4), scales=w_s[:, cols],
                                  in_=w_grp[:, cols, :].rearrange("p n t -> p (n t)"))

        def shifts():
            nc.vector.tensor_scalar(out=blk[:], in0=sq[:], scalar1=0.0, scalar2=None, op0=mybir.AluOpType.is_equal)
            for q in range(4):
                rows = slice(32 * q, 32 * q + 32)
                nc.vector.tensor_copy(out=id32[rows, 32 * q:32 * q + 32], in_=blk[rows, :])
            nc.vector.tensor_copy(out=cyc_up[:, 4:128], in_=id32[:, 0:124])
            nc.vector.tensor_copy(out=cyc_up[:, 0:4], in_=id32[:, 124:128])
            nc.vector.tensor_copy(out=cyc_dn[:, 0:124], in_=id32[:, 4:128])
            nc.vector.tensor_copy(out=cyc_dn[:, 124:128], in_=id32[:, 0:4])

        def border_rows_sum():
            acc_f = ps_a.tile([P, n_t, P], F32, tag="accz")
            for t in range(n_t):
                f = slice(t, n_feat, n_t)
                nc.tensor.matmul(acc_f[:, t, 0:64], lhsT=xf[:, f],
                                 rhs=adj[:, 0:192].rearrange("p (b j) -> p b j", b=6)[:, 1:5:3, :], start=True, stop=True)
            return acc_f

        def border_rows_round(acc_f):
            for rr in range(2):
                nc.scalar.copy(out=fix[:, :, rr, :, :],
                               in_=acc_f[:, :, 32 * rr:32 * rr + 32].rearrange("p t (q i) -> p i q t", q=4))

        def row_sums(ci):
            t32 = ts_pool.tile([P, n_feat], F32, tag="t32")
            s32 = ts_pool.tile([P, n_feat], F32, tag="s32")
            by_t = lambda row: row.rearrange("p (m t) -> p t m", t=n_t)
            t_out = t32[:].rearrange("p (t m) -> p t m", t=n_t)
            s_out = s32[:].rearrange("p (t m) -> p t m", t=n_t)
            nc.vector.tensor_tensor(out=t_out, in0=by_t(xz[:, ci, :]), in1=by_t(xz[:, ci + 2, :]), op=ADD)
            nc.vector.tensor_tensor(out=s_out, in0=t_out, in1=by_t(xz[:, ci + 1, :]), op=ADD)
            return t32, s32

        def z_sum(acc, t32, s32):
            for t in range(n_t):
                f = slice(P * t, P * t + P)
                nc.tensor.matmul(acc[:, t, :], lhsT=t32[:, f], rhs=id32[:], is_transpose=True, start=True, stop=False)
                nc.tensor.matmul(acc[:, t, :], lhsT=s32[:, f], rhs=cyc_up[:], is_transpose=True, start=False, stop=False)
                nc.tensor.matmul(acc[:, t, :], lhsT=s32[:, f], rhs=cyc_dn[:], is_transpose=True, start=False, stop=True)

        def p_parts(n):
            img = n // 8
            u = n % 8
            if u < 7:
                return [(x0, 8 * img + u, 64, 0, 64), (x2, 7 * img + u, 192, 64, 64)]
            return [(x0, 8 * img, 32, 0, 32), (x0, 8 * img + 7, 64, 32, 96)]

        def p_sum(acc, a, n):
            for t in range(n_t):
                f = slice(t, n_feat, n_t)
                for (src, blk, a_lo, o_lo, width) in p_parts(n):
                    nc.tensor.matmul(acc[:, a, t, o_lo:o_lo + width], lhsT=src[:, blk, f], rhs=adj[:, a_lo:a_lo + width],
                                     start=True, stop=True)

        def p_stores(n):
            img = n // 8
            u = n % 8
            if u < 7:
                return [(0, P, out[img, P * u + 32:P * u + 160, :])]
            return [(0, 32, out[img, 0:32, :]), (32, 96, out[img, 928:992, :]), (96, P, out[img, 992:1024, :])]

        pairs = []
        first_use = {}
        n_p = 0
        n_z = 0
        for s, kind in enumerate(PAIR_KINDS):
            if kind == "A":
                pairs.append([("p", n_p), ("p", n_p + 1)])
                n_p += 2
            else:
                pairs.append([("p", n_p), ("z", n_z)])
                first_use[s] = n_z
                n_p += 1
                n_z += 1

        def pair_tiles(s):
            return pairs[s]

        def strips_of(s):
            tiles = [(n // 8, n % 8) for kind, n in pair_tiles(s) if kind == "p" and n % 8 < 7]
            if len(tiles) == 2 and tiles[0][0] == tiles[1][0]:
                return [(tiles[0][0], tiles[0][1], tiles[1][1] + 1)]
            return [(img, u, u + 1) for img, u in tiles]

        def neighbour_sums(s, sums):
            acc_p = ps_a.tile([P, 2, n_t, P], BF16, tag="accp")
            acc_z = None
            for a, (kind, n) in enumerate(pair_tiles(s)):
                if kind == "p":
                    p_sum(acc_p, a, n)
                else:
                    acc_z = ps_a.tile([P, n_t, P], F32, tag="accz")
                    z_sum(acc_z, sums[n][0], sums[n][1])
            return acc_p, acc_z

        def round_out(s, accs, grp):
            acc_p, acc_z = accs
            if acc_z is None:
                nc.scalar.copy(out=grp[:], in_=acc_p[:].rearrange("p a t n -> p a n t"))
            else:
                n = pair_tiles(s)[1][1]
                nc.scalar.copy(out=grp[:, 0, :, :], in_=acc_p[:, 0, :, :].rearrange("p t n -> p n t"))
                nc.scalar.copy(out=grp[:, 1, :, :], in_=acc_z[:].rearrange("p t n -> p n t"))
                nc.scalar.copy(out=grp[:, 1, 0:4, :], in_=fix[:, n, 0, :, :])
                nc.scalar.copy(out=grp[:, 1, 124:128, :], in_=fix[:, n, 1, :, :])

        def quantise(grp):
            a_q = work.tile([P, 2 * P], U32, align_bytes=64, tag="a_q")
            a_s = work.tile([P, 2 * P], U8, align_bytes=64, tag="a_s")
            nc.vector.quantize_mx(out=a_q[:].bitcast(FP8X4), scales=a_s[:],
                                  in_=grp[:].rearrange("p a n t -> p (a n t)"))
            return a_q, a_s

        def multiply(a_q, a_s):
            banks = []
            for h in range(2):
                cols = slice(512 * h, 512 * h + 512)
                for a in range(2):
                    nodes = slice(P * a, P * a + P)
                    po = ps_o.tile([P, 512], F32, tag="po", name="po%d%d" % (h, a))
                    nc.tensor.matmul_mx(out=po[:], lhsT=a_q[:, nodes].bitcast(FP8X4), lhsT_scale=a_s[:, nodes],
                                        rhs=w_q[:, cols].bitcast(FP8X4), rhs_scale=w_s[:, cols],
                                        start=True, stop=True)
                    banks.append(po)
            return banks

        def out_tiles():
            o_tiles = []
            for a in range(2):
                o_new = stage.tile([P, n_out], F32, tag="o_sb", name="o_sb%d" % a)
                o_tiles.append(o_new)
            return o_tiles

        def add_bias(k, banks, o_tiles):
            cols = slice(512 * (k // 2), 512 * (k // 2) + 512)
            o_sb = o_tiles[k % 2]
            if k in G_HALVES:
                nc.scalar.copy(out=o_sb[:, cols], in_=banks[k][:])
                nc.gpsimd.tensor_tensor(out=o_sb[:, cols], in0=o_sb[:, cols], in1=b_bc[:, cols], op=ADD)
            else:
                nc.vector.tensor_tensor(out=o_sb[:, cols], in0=banks[k][:], in1=b_bc[:, cols], op=ADD)

        def store(s, a, o_tiles):
            kind, n = pair_tiles(s)[a]
            if kind == "z":
                nc.sync.dma_start(out=oz_view[:, n, :], in_=o_tiles[a][:])
            else:
                for (lo, hi, dest) in p_stores(n):
                    nc.sync.dma_start(out=dest, in_=o_tiles[a][lo:hi, :])

        n_pairs = len(PAIR_KINDS)
        sums = {}
        shifts()
        regroup(nc.vector.tensor_copy, 0, 512)
        weights_q(0)
        accs = neighbour_sums(0, sums)
        grp_next = work.tile([P, 2, P, n_t], BF16, align_bytes=64, tag="grp")
        round_out(0, accs, grp_next)
        fill_x2(nc.scalar.copy, 0, 2, 4)
        regroup(nc.scalar.copy, 768, 1024)
        fill_x2(nc.scalar.copy, 0, 4, 6)
        regroup(nc.vector.tensor_copy, 512, 768)
        ready = quantise(grp_next)
        weights_q(1)
        sums_after = {}
        for s in sorted(first_use):
            sums_after[max(s - 4, 0)] = first_use[s]
        for s in range(n_pairs):
            more = s + 1 < n_pairs
            if more:
                accs = neighbour_sums(s + 1, sums)
            banks = multiply(ready[0], ready[1])
            if s == 1:
                acc_f = border_rows_sum()
            o_tiles = out_tiles()
            if more:
                grp_next = work.tile([P, 2, P, n_t], BF16, align_bytes=64, tag="grp")
                round_out(s + 1, accs, grp_next)
                ready = quantise(grp_next)
            add_bias(0, banks, o_tiles)
            if s + 3 < n_pairs:
                for (img, lo, hi) in strips_of(s + 3):
                    fill_x2(nc.scalar.copy, img, lo, hi)
            if s == 1:
                border_rows_round(acc_f)
            add_bias(1, banks, o_tiles)
            add_bias(2, banks, o_tiles)
            store(s, 0, o_tiles)
            add_bias(3, banks, o_tiles)
            store(s, 1, o_tiles)
            if s in later_loads:
                load_half_image(later_loads[s][0], later_loads[s][1])
            if s in sums_after:
                sums[sums_after[s]] = row_sums(sums_after[s])
